import numpy as np
import ml_dtypes


def mxq(x, axis, fmt="e4m3"):
    dtype, down = {"e4m3": (ml_dtypes.float8_e4m3fn, 7), "e5m2": (ml_dtypes.float8_e5m2, 14)}[fmt]
    v = np.moveaxis(np.asarray(x, np.float32).astype(ml_dtypes.bfloat16).astype(np.float64), axis, -1)
    blocks = v.reshape(v.shape[:-1] + (-1, 32))
    amax = np.abs(blocks).max(-1, keepdims=True)
    byte = np.maximum(np.where(amax > 0, np.frexp(amax)[1] - 1 + 127, 0) - down, 1)
    scale = np.exp2(byte - 127.0)
    codes = (blocks / scale).astype(np.float32).astype(dtype).astype(np.float64)
    return np.moveaxis((codes * scale).reshape(v.shape), -1, axis)


WIDE = False


def mx_kscale(k):
    if not WIDE:
        return np.ones(k)
    levels = np.array([20, -20, 10, -10, 0])
    a = np.random.permutation(np.resize(levels, k // 512 * 4)).reshape(k // 512, 4)
    idx = np.arange(k)
    return np.exp2(a[idx // 512, idx % 128 // 32])


BF16 = ml_dtypes.bfloat16


def bf(x):
    return np.asarray(x, np.float32).astype(BF16)


def f64(x):
    return np.asarray(x).astype(np.float64)


B, S, K, N = 4, 256, 1024, 4096
T = B * S


def setup_inputs():
    s = mx_kscale(T).reshape(B, S, 1)
    inp = np.random.standard_normal((B, S, K)) * s
    weight = np.random.standard_normal((K, N)) * 0.03
    bias = np.random.standard_normal(N)
    g = np.random.standard_normal((B, S, N)) * np.exp2(np.random.randint(-12, 1, (B, S, 1))) * 4.0 / s
    return {"inp": bf(inp), "weight": bf(weight), "bias": bf(bias), "grad_out": bf(g)}


def reference(inp, weight, bias, grad_out):
    x = f64(inp).reshape(-1, inp.shape[-1])
    g = f64(grad_out).reshape(-1, grad_out.shape[-1])
    return mxq(x, 0, "e4m3").T @ mxq(g, 0, "e5m2")

@@ -1,0 +1,145 @@
+from contextlib import ExitStack
+
+import concourse.mybir as mybir
+
+BF16 = mybir.dt.bfloat16
+F32 = mybir.dt.float32
+U32 = mybir.dt.uint32
+U8 = mybir.dt.uint8
+E4M3 = mybir.dt.float8_e4m3fn_x4
+E5M2 = mybir.dt.float8_e5m2_x4
+
+P = 128
+PACK = 4
+K_PASS = P * PACK
+T = 1024
+M = 1024
+N = 4096
+PASSES = T // K_PASS
+UNIT = 512
+M_TILES = M // P
+N_TILES = N // UNIT
+
+FLOPS = 2 * T * M * N
+BYTES = 2 * T * M + 2 * T * N + 4 * M * N
+
+LOAD_GROUPS = ((0, 1024), (1024, 1024), (2048, 2048))
+STORE_TILES = 2
+
+
+def tile_fp8dynamiclinear_kernel(tc, inp, weight, bias, grad_out, out):
+    nc = tc.nc
+    x = inp.flatten_outer_dims()
+    g = grad_out.flatten_outer_dims()
+
+    with ExitStack() as ctx:
+        raw = ctx.enter_context(tc.tile_pool(name="raw", bufs=1))
+        keep = ctx.enter_context(tc.tile_pool(name="keep", bufs=1))
+        stage = ctx.enter_context(tc.tile_pool(name="stage", bufs=3))
+        outs = ctx.enter_context(tc.tile_pool(name="outs", bufs=16))
+        psum = ctx.enter_context(tc.psum_pool(name="psum", bufs=8))
+        ctx.enter_context(tc.manual_schedule())
+
+        x_raw = []
+        for c in range(PASSES):
+            t = raw.tile([P, PACK, M], BF16, name="x_raw%d" % c)
+            nc.sync.dma_start(
+                out=t[:],
+                in_=x[c * K_PASS : (c + 1) * K_PASS, :].rearrange("(p j) w -> p j w", j=PACK),
+            )
+            x_raw.append(t)
+        g_raw = {}
+        for gi, (col0, width) in enumerate(LOAD_GROUPS):
+            for c in range(PASSES):
+                t = raw.tile([P, PACK, width], BF16, name="g_raw%d_%d" % (gi, c))
+                nc.sync.dma_start(
+                    out=t[:],
+                    in_=g[c * K_PASS : (c + 1) * K_PASS, col0 : col0 + width].rearrange(
+                        "(p j) w -> p j w", j=PACK
+                    ),
+                )
+                g_raw[(gi, c)] = t
+
+        def g_source(nt, c):
+            col = nt * UNIT
+            for gi, (col0, width) in enumerate(LOAD_GROUPS):
+                if col0 <= col < col0 + width:
+                    return g_raw[(gi, c)][:, :, col - col0 : col - col0 + UNIT]
+            raise ValueError("no load group holds column %d" % col)
+
+        def x_source(xt, c):
+            return x_raw[c][:, :, xt * UNIT : (xt + 1) * UNIT]
+
+        units = {}
+
+        def open_unit(kind, idx):
+            grouped = stage.tile([P, PASSES, UNIT, PACK], BF16, tag="grouped", name="grouped_%s%d" % (kind, idx), align_bytes=64)
+            codes = keep.tile([P, PASSES, UNIT], U32, name="codes_%s%d" % (kind, idx), align_bytes=64)
+            scales = keep.tile([P, PASSES, UNIT], U8, name="scales_%s%d" % (kind, idx), align_bytes=64)
+            units[(kind, idx)] = (grouped, codes, scales)
+
+        def regroup(engine_copy, kind, idx, c):
+            if (kind, idx) not in units:
+                open_unit(kind, idx)
+            grouped = units[(kind, idx)][0]
+            src = x_source(idx, c) if kind == "x" else g_source(idx, c)
+            engine_copy(
+                out=grouped[:, c].rearrange("p (a i) t -> p a t i", i=4),
+                in_=src.rearrange("p t (a i) -> p a t i", i=4),
+            )
+
+        def quantise(kind, idx):
+            grouped, codes, scales = units[(kind, idx)]
+            nc.vector.quantize_mx(
+                out=codes[:].rearrange("p c w -> p (c w)").bitcast(E4M3 if kind == "x" else E5M2),
+                scales=scales[:].rearrange("p c w -> p (c w)"),
+                in_=grouped[:].rearrange("p c w t -> p (c w t)"),
+            )
+
+        vcopy = nc.vector.tensor_copy
+        scopy = nc.scalar.copy
+
+        regroup(vcopy, "x", 0, 0)
+        regroup(scopy, "x", 1, 0)
+        regroup(vcopy, "x", 0, 1)
+        regroup(scopy, "x", 1, 1)
+        quantise("x", 0)
+        regroup(vcopy, "g", 0, 0)
+        quantise("x", 1)
+        regroup(vcopy, "g", 0, 1)
+        quantise("g", 0)
+        regroup(vcopy, "g", 1, 0)
+        regroup(vcopy, "g", 1, 1)
+        for nt in range(2, N_TILES):
+            regroup(vcopy, "g", nt, 0)
+            quantise("g", nt - 1)
+            regroup(vcopy, "g", nt, 1)
+        quantise("g", N_TILES - 1)
+
+        for grp0 in range(0, N_TILES, STORE_TILES):
+            rows = {}
+            for nt in range(grp0, grp0 + STORE_TILES):
+                for m in range(M_TILES):
+                    if nt == grp0:
+                        rows[m] = outs.tile([P, STORE_TILES * UNIT], F32, tag="rows", name="rows_%d_%d" % (grp0, m))
+                    xc, xs = units[("x", m // 4)][1:]
+                    gc, gs = units[("g", nt)][1:]
+                    ms = slice((m % 4) * P, (m % 4 + 1) * P)
+                    acc = psum.tile([P, UNIT], F32, tag="acc", name="acc_%d_%d" % (nt, m))
+                    for c in range(PASSES):
+                        nc.tensor.matmul_mx(
+                            out=acc[:],
+                            lhsT=xc[:, c, ms].bitcast(E4M3),
+                            lhsT_scale=xs[:, c, ms],
+                            rhs=gc[:, c, :].bitcast(E5M2),
+                            rhs_scale=gs[:, c, :],
+                            start=(c == 0),
+                            stop=(c == PASSES - 1),
+                        )
+                    part = nt - grp0
+                    nc.scalar.copy(out=rows[m][:, part * UNIT : (part + 1) * UNIT], in_=acc[:])
+                    if nt == grp0 + STORE_TILES - 1:
+                        nc.sync.dma_start(
+                            out=out[m * P : (m + 1) * P, grp0 * UNIT : (grp0 + STORE_TILES) * UNIT],
+                            in_=rows[m][:],
+                        )

@@ -23,8 +23,10 @@ N_TILES = N // UNIT
 FLOPS = 2 * T * M * N
 BYTES = 2 * T * M + 2 * T * N + 4 * M * N
 
+KIB = 1024
 LOAD_GROUPS = ((0, 1024), (1024, 1024), (2048, 2048))
-STORE_TILES = 2
+PIECES = ((0, 2), (2, 2), (4, 4))
+VECTOR_HELPS_FROM = 44
 
 
 def tile_fp8dynamiclinear_kernel(tc, inp, weight, bias, grad_out, out):
@@ -33,25 +35,26 @@ def tile_fp8dynamiclinear_kernel(tc, inp, weight, bias, grad_out, out):
     g = grad_out.flatten_outer_dims()
 
     with ExitStack() as ctx:
-        raw = ctx.enter_context(tc.tile_pool(name="raw", bufs=1))
+        big = ctx.enter_context(tc.tile_pool(name="big", bufs=1))
         keep = ctx.enter_context(tc.tile_pool(name="keep", bufs=1))
-        stage = ctx.enter_context(tc.tile_pool(name="stage", bufs=3))
-        outs = ctx.enter_context(tc.tile_pool(name="outs", bufs=16))
+        stage = ctx.enter_context(tc.tile_pool(name="stage", bufs=4))
         psum = ctx.enter_context(tc.psum_pool(name="psum", bufs=8))
         ctx.enter_context(tc.manual_schedule())
 
         x_raw = []
         for c in range(PASSES):
-            t = raw.tile([P, PACK, M], BF16, name="x_raw%d" % c)
+            t = big.tile([P, PACK, M], BF16, name="x_raw%d" % c, offset=c * 8 * KIB)
             nc.sync.dma_start(
                 out=t[:],
                 in_=x[c * K_PASS : (c + 1) * K_PASS, :].rearrange("(p j) w -> p j w", j=PACK),
             )
             x_raw.append(t)
         g_raw = {}
+        place = 16 * KIB
         for gi, (col0, width) in enumerate(LOAD_GROUPS):
             for c in range(PASSES):
-                t = raw.tile([P, PACK, width], BF16, name="g_raw%d_%d" % (gi, c))
+                t = big.tile([P, PACK, width], BF16, name="g_raw%d_%d" % (gi, c), offset=place)
+                place += PACK * width * 2
                 nc.sync.dma_start(
                     out=t[:],
                     in_=g[c * K_PASS : (c + 1) * K_PASS, col0 : col0 + width].rearrange(
@@ -59,6 +62,13 @@ def tile_fp8dynamiclinear_kernel(tc, inp, weight, bias, grad_out, out):
                     ),
                 )
                 g_raw[(gi, c)] = t
+
+        def rows_offset(piece, m):
+            if piece == 0:
+                return (80 + 4 * m) * KIB
+            if piece == 1:
+                return (112 + 4 * m) * KIB
+            return 8 * m * KIB if m < 6 else (80 + 8 * (m - 6)) * KIB
 
         def g_source(nt, c):
             col = nt * UNIT
@@ -105,41 +115,65 @@ def tile_fp8dynamiclinear_kernel(tc, inp, weight, bias, grad_out, out):
         regroup(scopy, "x", 1, 1)
         quantise("x", 0)
         regroup(vcopy, "g", 0, 0)
+        regroup(scopy, "g", 1, 0)
         quantise("x", 1)
         regroup(vcopy, "g", 0, 1)
+        regroup(scopy, "g", 1, 1)
         quantise("g", 0)
-        regroup(vcopy, "g", 1, 0)
-        regroup(vcopy, "g", 1, 1)
-        for nt in range(2, N_TILES):
-            regroup(vcopy, "g", nt, 0)
-            quantise("g", nt - 1)
-            regroup(vcopy, "g", nt, 1)
-        quantise("g", N_TILES - 1)
+        regroup(vcopy, "g", 2, 0)
+        quantise("g", 1)
+        regroup(vcopy, "g", 2, 1)
+        regroup(vcopy, "g", 3, 0)
+        quantise("g", 2)
+        regroup(vcopy, "g", 3, 1)
+        regroup(vcopy, "g", 4, 0)
+        quantise("g", 3)
+        regroup(vcopy, "g", 5, 0)
+        regroup(vcopy, "g", 6, 0)
+        regroup(vcopy, "g", 7, 0)
+        regroup(vcopy, "g", 4, 1)
+        regroup(vcopy, "g", 5, 1)
+        quantise("g", 4)
+        regroup(vcopy, "g", 6, 1)
+        quantise("g", 5)
+        regroup(vcopy, "g", 7, 1)
+        quantise("g", 6)
+        quantise("g", 7)
 
-        for grp0 in range(0, N_TILES, STORE_TILES):
-            rows = {}
-            for nt in range(grp0, grp0 + STORE_TILES):
-                for m in range(M_TILES):
-                    if nt == grp0:
-                        rows[m] = outs.tile([P, STORE_TILES * UNIT], F32, tag="rows", name="rows_%d_%d" % (grp0, m))
-                    xc, xs = units[("x", m // 4)][1:]
-                    gc, gs = units[("g", nt)][1:]
-                    ms = slice((m % 4) * P, (m % 4 + 1) * P)
-                    acc = psum.tile([P, UNIT], F32, tag="acc", name="acc_%d_%d" % (nt, m))
-                    for c in range(PASSES):
-                        nc.tensor.matmul_mx(
-                            out=acc[:],
-                            lhsT=xc[:, c, ms].bitcast(E4M3),
-                            lhsT_scale=xs[:, c, ms],
-                            rhs=gc[:, c, :].bitcast(E5M2),
-                            rhs_scale=gs[:, c, :],
-                            start=(c == 0),
-                            stop=(c == PASSES - 1),
-                        )
-                    part = nt - grp0
-                    nc.scalar.copy(out=rows[m][:, part * UNIT : (part + 1) * UNIT], in_=acc[:])
-                    if nt == grp0 + STORE_TILES - 1:
-                        nc.sync.dma_start(
-                            out=out[m * P : (m + 1) * P, grp0 * UNIT : (grp0 + STORE_TILES) * UNIT],
-                            in_=rows[m][:],
-                        )
+        order = []
+        for piece, (first, count) in enumerate(PIECES):
+            tiles = range(first, first + count)
+            if count == 2:
+                order.extend([(piece, nt, m) for nt in tiles for m in range(M_TILES)])
+            else:
+                order.extend([(piece, nt, m) for nt in tiles for m in range(2)])
+                order.extend([(piece, nt, m) for m in range(2, M_TILES) for nt in tiles])
+
+        rows = {}
+        for n, (piece, nt, m) in enumerate(order):
+            first, count = PIECES[piece]
+            if (piece, m) not in rows:
+                rows[(piece, m)] = big.tile([P, count * UNIT], F32, name="rows_%d_%d" % (piece, m), offset=rows_offset(piece, m))
+            row = rows[(piece, m)]
+            xc, xs = units[("x", m // 4)][1:]
+            gc, gs = units[("g", nt)][1:]
+            ms = slice((m % 4) * P, (m % 4 + 1) * P)
+            acc = psum.tile([P, UNIT], F32, tag="acc", name="acc_%d_%d" % (nt, m))
+            for c in range(PASSES):
+                nc.tensor.matmul_mx(
+                    out=acc[:],
+                    lhsT=xc[:, c, ms].bitcast(E4M3),
+                    lhsT_scale=xs[:, c, ms],
+                    rhs=gc[:, c, :].bitcast(E5M2),
+                    rhs_scale=gs[:, c, :],
+                    start=(c == 0),
+                    stop=(c == PASSES - 1),
+                )
+            part = nt - first
+            empty = vcopy if (n >= VECTOR_HELPS_FROM and n % 2 == 1) else scopy
+            empty(out=row[:, part * UNIT : (part + 1) * UNIT], in_=acc[:])
+            if part == count - 1:
+                nc.sync.dma_start(
+                    out=out[m * P : (m + 1) * P, first * UNIT : (first + count) * UNIT],
+                    in_=row[:],
+                )

from contextlib import ExitStack

import concourse.mybir as mybir

BF16 = mybir.dt.bfloat16
F32 = mybir.dt.float32
U32 = mybir.dt.uint32
U8 = mybir.dt.uint8
E4M3 = mybir.dt.float8_e4m3fn_x4
E5M2 = mybir.dt.float8_e5m2_x4

P = 128
PACK = 4
K_PASS = P * PACK
T = 1024
M = 1024
N = 4096
PASSES = T // K_PASS
UNIT = 512
M_TILES = M // P
N_TILES = N // UNIT

FLOPS = 2 * T * M * N
BYTES = 2 * T * M + 2 * T * N + 4 * M * N

KIB = 1024
LOAD_GROUPS = ((0, 1024), (1024, 1024), (2048, 2048))
PIECES = ((0, 2), (2, 2), (4, 4))
VECTOR_HELPS_FROM = 44


def tile_fp8dynamiclinear_kernel(tc, inp, weight, bias, grad_out, out):
    nc = tc.nc
    x = inp.flatten_outer_dims()
    g = grad_out.flatten_outer_dims()

    with ExitStack() as ctx:
        big = ctx.enter_context(tc.tile_pool(name="big", bufs=1))
        keep = ctx.enter_context(tc.tile_pool(name="keep", bufs=1))
        stage = ctx.enter_context(tc.tile_pool(name="stage", bufs=4))
        psum = ctx.enter_context(tc.psum_pool(name="psum", bufs=8))
        ctx.enter_context(tc.manual_schedule())

        x_raw = []
        for c in range(PASSES):
            t = big.tile([P, PACK, M], BF16, name="x_raw%d" % c, offset=c * 8 * KIB)
            nc.sync.dma_start(
                out=t[:],
                in_=x[c * K_PASS : (c + 1) * K_PASS, :].rearrange("(p j) w -> p j w", j=PACK),
            )
            x_raw.append(t)
        g_raw = {}
        place = 16 * KIB
        for gi, (col0, width) in enumerate(LOAD_GROUPS):
            for c in range(PASSES):
                t = big.tile([P, PACK, width], BF16, name="g_raw%d_%d" % (gi, c), offset=place)
                place += PACK * width * 2
                nc.sync.dma_start(
                    out=t[:],
                    in_=g[c * K_PASS : (c + 1) * K_PASS, col0 : col0 + width].rearrange(
                        "(p j) w -> p j w", j=PACK
                    ),
                )
                g_raw[(gi, c)] = t

        def rows_offset(piece, m):
            if piece == 0:
                return (80 + 4 * m) * KIB
            if piece == 1:
                return (112 + 4 * m) * KIB
            return 8 * m * KIB if m < 6 else (80 + 8 * (m - 6)) * KIB

        def g_source(nt, c):
            col = nt * UNIT
            for gi, (col0, width) in enumerate(LOAD_GROUPS):
                if col0 <= col < col0 + width:
                    return g_raw[(gi, c)][:, :, col - col0 : col - col0 + UNIT]
            raise ValueError("no load group holds column %d" % col)

        def x_source(xt, c):
            return x_raw[c][:, :, xt * UNIT : (xt + 1) * UNIT]

        units = {}

        def open_unit(kind, idx):
            grouped = stage.tile([P, PASSES, UNIT, PACK], BF16, tag="grouped", name="grouped_%s%d" % (kind, idx), align_bytes=64)
            codes = keep.tile([P, PASSES, UNIT], U32, name="codes_%s%d" % (kind, idx), align_bytes=64)
            scales = keep.tile([P, PASSES, UNIT], U8, name="scales_%s%d" % (kind, idx), align_bytes=64)
            units[(kind, idx)] = (grouped, codes, scales)

        def regroup(engine_copy, kind, idx, c):
            if (kind, idx) not in units:
                open_unit(kind, idx)
            grouped = units[(kind, idx)][0]
            src = x_source(idx, c) if kind == "x" else g_source(idx, c)
            engine_copy(
                out=grouped[:, c].rearrange("p (a i) t -> p a t i", i=4),
                in_=src.rearrange("p t (a i) -> p a t i", i=4),
            )

        def quantise(kind, idx):
            grouped, codes, scales = units[(kind, idx)]
            nc.vector.quantize_mx(
                out=codes[:].rearrange("p c w -> p (c w)").bitcast(E4M3 if kind == "x" else E5M2),
                scales=scales[:].rearrange("p c w -> p (c w)"),
                in_=grouped[:].rearrange("p c w t -> p (c w t)"),
            )

        vcopy = nc.vector.tensor_copy
        scopy = nc.scalar.copy

        regroup(vcopy, "x", 0, 0)
        regroup(scopy, "x", 1, 0)
        regroup(vcopy, "x", 0, 1)
        regroup(scopy, "x", 1, 1)
        quantise("x", 0)
        regroup(vcopy, "g", 0, 0)
        regroup(scopy, "g", 1, 0)
        quantise("x", 1)
        regroup(vcopy, "g", 0, 1)
        regroup(scopy, "g", 1, 1)
        quantise("g", 0)
        regroup(vcopy, "g", 2, 0)
        quantise("g", 1)
        regroup(vcopy, "g", 2, 1)
        regroup(vcopy, "g", 3, 0)
        quantise("g", 2)
        regroup(vcopy, "g", 3, 1)
        regroup(vcopy, "g", 4, 0)
        quantise("g", 3)
        regroup(vcopy, "g", 5, 0)
        regroup(vcopy, "g", 6, 0)
        regroup(vcopy, "g", 7, 0)
        regroup(vcopy, "g", 4, 1)
        regroup(vcopy, "g", 5, 1)
        quantise("g", 4)
        regroup(vcopy, "g", 6, 1)
        quantise("g", 5)
        regroup(vcopy, "g", 7, 1)
        quantise("g", 6)
        quantise("g", 7)

        order = []
        for piece, (first, count) in enumerate(PIECES):
            tiles = range(first, first + count)
            if count == 2:
                order.extend([(piece, nt, m) for nt in tiles for m in range(M_TILES)])
            else:
                order.extend([(piece, nt, m) for nt in tiles for m in range(2)])
                order.extend([(piece, nt, m) for m in range(2, M_TILES) for nt in tiles])

        rows = {}
        for n, (piece, nt, m) in enumerate(order):
            first, count = PIECES[piece]
            if (piece, m) not in rows:
                rows[(piece, m)] = big.tile([P, count * UNIT], F32, name="rows_%d_%d" % (piece, m), offset=rows_offset(piece, m))
            row = rows[(piece, m)]
            xc, xs = units[("x", m // 4)][1:]
            gc, gs = units[("g", nt)][1:]
            ms = slice((m % 4) * P, (m % 4 + 1) * P)
            acc = psum.tile([P, UNIT], F32, tag="acc", name="acc_%d_%d" % (nt, m))
            for c in range(PASSES):
                nc.tensor.matmul_mx(
                    out=acc[:],
                    lhsT=xc[:, c, ms].bitcast(E4M3),
                    lhsT_scale=xs[:, c, ms],
                    rhs=gc[:, c, :].bitcast(E5M2),
                    rhs_scale=gs[:, c, :],
                    start=(c == 0),
                    stop=(c == PASSES - 1),
                )
            part = nt - first
            empty = vcopy if (n >= VECTOR_HELPS_FROM and n % 2 == 1) else scopy
            empty(out=row[:, part * UNIT : (part + 1) * UNIT], in_=acc[:])
            if part == count - 1:
                nc.sync.dma_start(
                    out=out[m * P : (m + 1) * P, first * UNIT : (first + count) * UNIT],
                    in_=row[:],
                )
